import numpy as np
import ml_dtypes


def mxq(x, axis, fmt="e4m3"):
    dtype, down = {"e4m3": (ml_dtypes.float8_e4m3fn, 7), "e5m2": (ml_dtypes.float8_e5m2, 14)}[fmt]
    v = np.moveaxis(np.asarray(x, np.float32).astype(ml_dtypes.bfloat16).astype(np.float64), axis, -1)
    blocks = v.reshape(v.shape[:-1] + (-1, 32))
    amax = np.abs(blocks).max(-1, keepdims=True)
    byte = np.maximum(np.where(amax > 0, np.frexp(amax)[1] - 1 + 127, 0) - down, 1)
    scale = np.exp2(byte - 127.0)
    codes = (blocks / scale).astype(np.float32).astype(dtype).astype(np.float64)
    return np.moveaxis((codes * scale).reshape(v.shape), -1, axis)


BF16 = ml_dtypes.bfloat16


def bf(x):
    return np.asarray(x, np.float32).astype(BF16)


def f64(x):
    return np.asarray(x).astype(np.float64)


N, D, C = 512, 4096, 4


def unit(v):
    return v / np.linalg.norm(v, axis=-1, keepdims=True)


def cnormal(*shape):
    return np.random.standard_normal(shape) + 1j * np.random.standard_normal(shape)


def draw_states():
    centre = unit(unit(cnormal(D)) + unit(cnormal(C, D)))
    label = np.random.randint(0, C, N)
    a2 = np.where(np.random.random(N) < 0.5, 0.95, 0.65)[:, None]
    psi = np.sqrt(a2) * centre[label] + np.sqrt(1.0 - a2) * unit(cnormal(N, D))
    theta = 2.0 * np.pi * np.random.random(N)[:, None]
    return unit(psi * np.exp(1j * theta))


def setup_inputs():
    psi = draw_states()
    return {"latent_re": bf(psi.real), "latent_im": bf(psi.imag)}


def reference(latent_re, latent_im):
    rq = mxq(f64(latent_re), 1, "e4m3")
    iq = mxq(f64(latent_im), 1, "e4m3")
    g_re = (rq @ rq.T) + (iq @ iq.T)
    g_im = (iq @ rq.T) - (rq @ iq.T)
    return g_re * g_re + g_im * g_im

@@ -1,0 +1,162 @@
+from contextlib import ExitStack
+
+import concourse.mybir as mybir
+from concourse.masks import make_identity
+
+F32 = mybir.dt.float32
+BF16 = mybir.dt.bfloat16
+U32 = mybir.dt.uint32
+U8 = mybir.dt.uint8
+FP8X4 = mybir.dt.float8_e4m3fn_x4
+SQUARE = mybir.ActivationFunctionType.Square
+
+P = 128
+N = 512
+D = 4096
+TILES = N // P
+PASSES = D // 512
+BANKS = 4
+FLOPS = 4 * 2 * N * N * D
+
+PARTS = {0: [(0, 128)], 1: [(0, 256)], 2: [(0, 256), (256, 384)], 3: [(0, 256), (256, 512)]}
+VECTOR_COPIES = (1, 3)
+
+
+def tile_quantumgraphneuralnetwork_pa_kernel(tc, latent_re, latent_im, out):
+    nc = tc.nc
+    latent = (latent_re, latent_im)
+    with ExitStack() as ctx:
+        keep = ctx.enter_context(tc.tile_pool(name="keep", bufs=1))
+        stage = ctx.enter_context(tc.tile_pool(name="stage", bufs=8))
+        epi = ctx.enter_context(tc.tile_pool(name="epi", bufs=2))
+        psum = ctx.enter_context(tc.psum_pool(name="psum", bufs=1))
+        ctx.enter_context(tc.manual_schedule())
+
+        x_sb = [[keep.tile([P, D], BF16, name="x%d_%d" % (s, j)) for j in range(TILES)] for s in range(2)]
+        codes = [keep.tile([P, PASSES, N], U32, name="codes%d" % s, align_bytes=64) for s in range(2)]
+        scales = [keep.tile([P, PASSES, N], U8, name="scales%d" % s, align_bytes=64) for s in range(2)]
+        out_sb = [keep.tile([P, N], F32, name="out_sb%d" % j) for j in range(TILES)]
+        ident = keep.tile([P, P], F32, name="ident")
+        warm = keep.tile([P, 2], F32, name="warm")
+
+        for s in range(2):
+            for c in range(4):
+                cols = slice(1024 * c, 1024 * c + 1024)
+                nc.sync.dma_start(out=x_sb[s][0][:, cols], in_=latent[s][0:P, cols])
+        for j in range(1, TILES):
+            for s in range(2):
+                nc.sync.dma_start(out=x_sb[s][j][:], in_=latent[s][P * j : P * j + P, :])
+
+        make_identity(nc, ident[:])
+        nc.vector.memset(warm[:, 0:1], 0.0)
+        nc.scalar.activation(out=warm[:, 1:2], in_=warm[:, 0:1], func=SQUARE)
+
+        def transposes(j, b):
+            s, q4 = divmod(b, BANKS)
+            words = x_sb[s][j][:].bitcast(F32)
+            tp = psum.tile([P, 4, P], F32, tag="tp", bufs=4, name="tp")
+            for q in range(4):
+                w0 = 512 * q4 + P * q
+                nc.tensor.transpose(tp[:, q, :], words[:, w0 : w0 + P], ident[:])
+            grouped = stage.tile([P, 1024], BF16, tag="grouped", name="grouped", align_bytes=64)
+            dst = grouped[:].bitcast(F32).rearrange("p (a n u) -> p a n u", a=2, u=2)
+            src = tp[:].rearrange("p (a u) n -> p a n u", u=2)
+            if b in VECTOR_COPIES:
+                nc.vector.tensor_copy(out=dst, in_=src)
+            else:
+                nc.scalar.copy(out=dst, in_=src)
+            return grouped
+
+        def quantise(j, b, grouped):
+            s, q4 = divmod(b, BANKS)
+            rows = slice(P * j, P * j + P)
+            for a in range(2):
+                g = 2 * q4 + a
+                nc.vector.quantize_mx(
+                    out=codes[s][:, g, rows].bitcast(FP8X4),
+                    scales=scales[s][:, g, rows],
+                    in_=grouped[:, 512 * a : 512 * a + 512],
+                )
+
+        def passes(acc, j, stat, mov, cols, first, last):
+            rows = slice(P * j, P * j + P)
+            for g in range(PASSES):
+                nc.tensor.matmul_mx(
+                    out=acc,
+                    lhsT=codes[stat][:, g, rows].bitcast(FP8X4),
+                    lhsT_scale=scales[stat][:, g, rows],
+                    rhs=codes[mov][:, g, cols].bitcast(FP8X4),
+                    rhs_scale=scales[mov][:, g, cols],
+                    start=(first and g == 0),
+                    stop=(last and g == PASSES - 1),
+                )
+
+        def products(j, c0, c1):
+            w = c1 - c0
+            cols = slice(c0, c1)
+            acc_g = psum.tile([P, N], F32, tag="acc_g", bufs=2, name="acc_g")
+            acc_b = psum.tile([P, N], F32, tag="acc_b", bufs=1, name="acc_b")
+            acc_a = psum.tile([P, N], F32, tag="acc_a", bufs=1, name="acc_a")
+            passes(acc_g[:, 0:w], j, 0, 0, cols, True, False)
+            passes(acc_b[:, 0:w], j, 0, 1, cols, True, True)
+            b_sb = epi.tile([P, N], F32, tag="b_sb", name="b_sb")
+            nc.scalar.copy(out=b_sb[:, 0:w], in_=acc_b[:, 0:w])
+            passes(acc_a[:, 0:w], j, 1, 0, cols, True, True)
+            diff = epi.tile([P, N], F32, tag="diff", name="diff")
+            nc.vector.tensor_sub(out=diff[:, 0:w], in0=acc_a[:, 0:w], in1=b_sb[:, 0:w])
+            sq_im = epi.tile([P, N], F32, tag="sq_im", name="sq_im")
+            nc.scalar.activation(out=sq_im[:, 0:w], in_=diff[:, 0:w], func=SQUARE)
+            passes(acc_g[:, 0:w], j, 1, 1, cols, False, True)
+            return acc_g, sq_im
+
+        def finish(j, c0, c1, acc_g, sq_im):
+            w = c1 - c0
+            sq_re = epi.tile([P, N], F32, tag="sq_re", name="sq_re")
+            nc.scalar.activation(out=sq_re[:, 0:w], in_=acc_g[:, 0:w], func=SQUARE)
+            nc.vector.tensor_add(out=out_sb[j][:, c0:c1], in0=sq_re[:, 0:w], in1=sq_im[:, 0:w])
+            nc.sync.dma_start(out=out[P * j : P * j + P, c0:c1], in_=out_sb[j][:, c0:c1])
+
+        def mirror(groups, on_vector):
+            mt = psum.tile([P, 4, P], F32, tag="tp", bufs=4, name="mt")
+            count = 0
+            for j, i0, i1 in groups:
+                for i in range(i0, i1):
+                    nc.tensor.transpose(mt[:, count, :], out_sb[j][:, P * i : P * i + P], ident[:])
+                    count += 1
+            m_sb = epi.tile([P, 4, P], F32, tag="m_sb", name="m_sb")
+            if on_vector:
+                nc.vector.tensor_copy(out=m_sb[:, 0:count, :], in_=mt[:, 0:count, :])
+            else:
+                nc.scalar.copy(out=m_sb[:, 0:count, :], in_=mt[:, 0:count, :])
+            count = 0
+            for j, i0, i1 in groups:
+                nc.sync.dma_start(
+                    out=out[P * i0 : P * i1, P * j : P * j + P].rearrange("(i p) c -> p i c", p=P),
+                    in_=m_sb[:, count : count + i1 - i0, :],
+                )
+                count += i1 - i0
+
+        pending = []
+        for j in range(TILES):
+            held = []
+            for b in range(BANKS):
+                held.append(transposes(j, b))
+            for b in range(BANKS):
+                quantise(j, b, held[b])
+            for b in range(BANKS, 2 * BANKS):
+                quantise(j, b, transposes(j, b))
+            if j == 3:
+                mirror([(1, 0, 1), (2, 0, 2)], True)
+            for args in pending:
+                finish(*args)
+            pending = []
+            for k, (c0, c1) in enumerate(PARTS[j]):
+                acc_g, sq_im = products(j, c0, c1)
+                if k == len(PARTS[j]) - 1:
+                    pending.append((j, c0, c1, acc_g, sq_im))
+                else:
+                    finish(j, c0, c1, acc_g, sq_im)
+        mirror([(3, 0, 2)], True)
+        for args in pending:
+            finish(*args)
+        mirror([(3, 2, 3)], False)

@@ -18,8 +18,13 @@ PASSES = D // 512
 BANKS = 4
 FLOPS = 4 * 2 * N * N * D
 
-PARTS = {0: [(0, 128)], 1: [(0, 256)], 2: [(0, 256), (256, 384)], 3: [(0, 256), (256, 512)]}
-VECTOR_COPIES = (1, 3)
+PROGRAM = {
+    0: [((0, 128), None, (0, 128))],
+    1: [((0, 256), (0, 128), (0, 256))],
+    2: [((0, 256), (0, 256), (0, 256)), ((256, 384), None, (256, 384))],
+    3: [((0, 256), (0, 256), (0, 256)), ((256, 384), (256, 384), (256, 512)), ((384, 512), None, None)],
+}
+VECTOR_COPIES = (1, 6)
 
 
 def tile_quantumgraphneuralnetwork_pa_kernel(tc, latent_re, latent_im, out):
@@ -36,6 +41,9 @@ def tile_quantumgraphneuralnetwork_pa_kernel(tc, latent_re, latent_im, out):
         codes = [keep.tile([P, PASSES, N], U32, name="codes%d" % s, align_bytes=64) for s in range(2)]
         scales = [keep.tile([P, PASSES, N], U8, name="scales%d" % s, align_bytes=64) for s in range(2)]
         out_sb = [keep.tile([P, N], F32, name="out_sb%d" % j) for j in range(TILES)]
+        sq_re = [keep.tile([P, N], F32, name="sq_re%d" % j) for j in range(TILES)]
+        sq_im = [keep.tile([P, N], F32, name="sq_im%d" % j) for j in range(TILES)]
+        a_diag = [keep.tile([P, P], F32, name="a_diag%d" % j) for j in range(TILES)]
         ident = keep.tile([P, P], F32, name="ident")
         warm = keep.tile([P, 2], F32, name="warm")
 
@@ -78,11 +86,12 @@ def tile_quantumgraphneuralnetwork_pa_kernel(tc, latent_re, latent_im, out):
                     in_=grouped[:, 512 * a : 512 * a + 512],
                 )
 
-        def passes(acc, j, stat, mov, cols, first, last):
+        def passes(acc, j, stat, mov, span, first, last):
             rows = slice(P * j, P * j + P)
+            cols = slice(span[0], span[1])
             for g in range(PASSES):
                 nc.tensor.matmul_mx(
-                    out=acc,
+                    out=acc[:, 0 : span[1] - span[0]],
                     lhsT=codes[stat][:, g, rows].bitcast(FP8X4),
                     lhsT_scale=scales[stat][:, g, rows],
                     rhs=codes[mov][:, g, cols].bitcast(FP8X4),
@@ -91,72 +100,71 @@ def tile_quantumgraphneuralnetwork_pa_kernel(tc, latent_re, latent_im, out):
                     stop=(last and g == PASSES - 1),
                 )
 
-        def products(j, c0, c1):
-            w = c1 - c0
-            cols = slice(c0, c1)
-            acc_g = psum.tile([P, N], F32, tag="acc_g", bufs=2, name="acc_g")
-            acc_b = psum.tile([P, N], F32, tag="acc_b", bufs=1, name="acc_b")
-            acc_a = psum.tile([P, N], F32, tag="acc_a", bufs=1, name="acc_a")
-            passes(acc_g[:, 0:w], j, 0, 0, cols, True, False)
-            passes(acc_b[:, 0:w], j, 0, 1, cols, True, True)
-            b_sb = epi.tile([P, N], F32, tag="b_sb", name="b_sb")
-            nc.scalar.copy(out=b_sb[:, 0:w], in_=acc_b[:, 0:w])
-            passes(acc_a[:, 0:w], j, 1, 0, cols, True, True)
-            diff = epi.tile([P, N], F32, tag="diff", name="diff")
-            nc.vector.tensor_sub(out=diff[:, 0:w], in0=acc_a[:, 0:w], in1=b_sb[:, 0:w])
-            sq_im = epi.tile([P, N], F32, tag="sq_im", name="sq_im")
-            nc.scalar.activation(out=sq_im[:, 0:w], in_=diff[:, 0:w], func=SQUARE)
-            passes(acc_g[:, 0:w], j, 1, 1, cols, False, True)
-            return acc_g, sq_im
-
-        def finish(j, c0, c1, acc_g, sq_im):
-            w = c1 - c0
-            sq_re = epi.tile([P, N], F32, tag="sq_re", name="sq_re")
-            nc.scalar.activation(out=sq_re[:, 0:w], in_=acc_g[:, 0:w], func=SQUARE)
-            nc.vector.tensor_add(out=out_sb[j][:, c0:c1], in0=sq_re[:, 0:w], in1=sq_im[:, 0:w])
+        def store(j, c0, c1):
             nc.sync.dma_start(out=out[P * j : P * j + P, c0:c1], in_=out_sb[j][:, c0:c1])
 
-        def mirror(groups, on_vector):
-            mt = psum.tile([P, 4, P], F32, tag="tp", bufs=4, name="mt")
-            count = 0
-            for j, i0, i1 in groups:
-                for i in range(i0, i1):
-                    nc.tensor.transpose(mt[:, count, :], out_sb[j][:, P * i : P * i + P], ident[:])
-                    count += 1
-            m_sb = epi.tile([P, 4, P], F32, tag="m_sb", name="m_sb")
-            if on_vector:
-                nc.vector.tensor_copy(out=m_sb[:, 0:count, :], in_=mt[:, 0:count, :])
-            else:
-                nc.scalar.copy(out=m_sb[:, 0:count, :], in_=mt[:, 0:count, :])
-            count = 0
-            for j, i0, i1 in groups:
+        def extras(j):
+            ex = psum.tile([P, 4, P], F32, tag="acc_g", bufs=2, name="ex")
+            nc.tensor.transpose(ex[:, 0, :], a_diag[j][:], ident[:])
+            for i in range(j):
+                nc.tensor.transpose(ex[:, 1 + i, :], out_sb[j][:, P * i : P * i + P], ident[:])
+            diag = slice(P * j, P * j + P)
+            diff = epi.tile([P, P], F32, tag="diff_d", name="diff_d")
+            nc.vector.tensor_sub(out=diff[:], in0=a_diag[j][:], in1=ex[:, 0, :])
+            nc.vector.tensor_mul(out=sq_im[j][:, diag], in0=diff[:], in1=diff[:])
+            if j > 0:
+                m_sb = epi.tile([P, 3, P], F32, tag="m_sb", name="m_sb")
+                nc.scalar.copy(out=m_sb[:, 0:j, :], in_=ex[:, 1 : 1 + j, :])
                 nc.sync.dma_start(
-                    out=out[P * i0 : P * i1, P * j : P * j + P].rearrange("(i p) c -> p i c", p=P),
-                    in_=m_sb[:, count : count + i1 - i0, :],
+                    out=out[0 : P * j, diag].rearrange("(i p) c -> p i c", p=P),
+                    in_=m_sb[:, 0:j, :],
                 )
-                count += i1 - i0
 
-        pending = []
+        def finish_diag(j):
+            diag = slice(P * j, P * j + P)
+            nc.vector.tensor_add(out=out_sb[j][:, diag], in0=sq_re[j][:, diag], in1=sq_im[j][:, diag])
+            store(j, P * j, P * j + P)
+
         for j in range(TILES):
-            held = []
-            for b in range(BANKS):
-                held.append(transposes(j, b))
-            for b in range(BANKS):
-                quantise(j, b, held[b])
-            for b in range(BANKS, 2 * BANKS):
-                quantise(j, b, transposes(j, b))
-            if j == 3:
-                mirror([(1, 0, 1), (2, 0, 2)], True)
-            for args in pending:
-                finish(*args)
-            pending = []
-            for k, (c0, c1) in enumerate(PARTS[j]):
-                acc_g, sq_im = products(j, c0, c1)
-                if k == len(PARTS[j]) - 1:
-                    pending.append((j, c0, c1, acc_g, sq_im))
-                else:
-                    finish(j, c0, c1, acc_g, sq_im)
-        mirror([(3, 0, 2)], True)
-        for args in pending:
-            finish(*args)
-        mirror([(3, 2, 3)], False)
+            held = None
+            for b in range(2 * BANKS):
+                grouped = transposes(j, b)
+                if b > 0:
+                    quantise(j, b - 1, held)
+                held = grouped
+            quantise(j, 2 * BANKS - 1, held)
+            if j > 0:
+                extras(j - 1)
+                finish_diag(j - 1)
+            off = P * j
+            for g_span, b_span, a_span in PROGRAM[j]:
+                acc_g = psum.tile([P, N], F32, tag="acc_g", bufs=2, name="acc_g")
+                passes(acc_g, j, 0, 0, g_span, True, False)
+                if b_span is not None:
+                    wb = b_span[1] - b_span[0]
+                    acc_b = psum.tile([P, N], F32, tag="acc_b", bufs=1, name="acc_b")
+                    passes(acc_b, j, 0, 1, b_span, True, True)
+                    b_sb = epi.tile([P, N], F32, tag="b_sb", name="b_sb")
+                    nc.scalar.copy(out=b_sb[:, 0:wb], in_=acc_b[:, 0:wb])
+                if a_span is not None:
+                    acc_a = psum.tile([P, N], F32, tag="acc_a", bufs=1, name="acc_a")
+                    passes(acc_a, j, 1, 0, a_span, True, True)
+                    if b_span is not None:
+                        diff = epi.tile([P, N], F32, tag="diff", name="diff")
+                        nc.vector.tensor_sub(out=diff[:, 0:wb], in0=acc_a[:, 0:wb], in1=b_sb[:, 0:wb])
+                        nc.scalar.activation(out=sq_im[j][:, b_span[0] : b_span[1]], in_=diff[:, 0:wb], func=SQUARE)
+                    if a_span[1] > off:
+                        nc.vector.tensor_copy(out=a_diag[j][:], in_=acc_a[:, off - a_span[0] : off - a_span[0] + P])
+                if j == TILES - 1 and g_span[0] == off:
+                    extras(j)
+                passes(acc_g, j, 1, 1, g_span, False, True)
+                nc.scalar.activation(
+                    out=sq_re[j][:, g_span[0] : g_span[1]], in_=acc_g[:, 0 : g_span[1] - g_span[0]], func=SQUARE
+                )
+                c1 = min(g_span[1], off)
+                if c1 > g_span[0]:
+                    nc.vector.tensor_add(
+                        out=out_sb[j][:, g_span[0] : c1], in0=sq_re[j][:, g_span[0] : c1], in1=sq_im[j][:, g_span[0] : c1]
+                    )
+                    store(j, g_span[0], c1)
+        finish_diag(TILES - 1)

@@ -24,7 +24,7 @@ PROGRAM = {
     2: [((0, 256), (0, 256), (0, 256)), ((256, 384), None, (256, 384))],
     3: [((0, 256), (0, 256), (0, 256)), ((256, 384), (256, 384), (256, 512)), ((384, 512), None, None)],
 }
-VECTOR_COPIES = (1, 6)
+VECTOR_COPY = 1
 
 
 def tile_quantumgraphneuralnetwork_pa_kernel(tc, latent_re, latent_im, out):
@@ -59,8 +59,7 @@ def tile_quantumgraphneuralnetwork_pa_kernel(tc, latent_re, latent_im, out):
         nc.vector.memset(warm[:, 0:1], 0.0)
         nc.scalar.activation(out=warm[:, 1:2], in_=warm[:, 0:1], func=SQUARE)
 
-        def transposes(j, b):
-            s, q4 = divmod(b, BANKS)
+        def transposes(j, s, q4):
             words = x_sb[s][j][:].bitcast(F32)
             tp = psum.tile([P, 4, P], F32, tag="tp", bufs=4, name="tp")
             for q in range(4):
@@ -69,14 +68,13 @@ def tile_quantumgraphneuralnetwork_pa_kernel(tc, latent_re, latent_im, out):
             grouped = stage.tile([P, 1024], BF16, tag="grouped", name="grouped", align_bytes=64)
             dst = grouped[:].bitcast(F32).rearrange("p (a n u) -> p a n u", a=2, u=2)
             src = tp[:].rearrange("p (a u) n -> p a n u", u=2)
-            if b in VECTOR_COPIES:
+            if q4 == VECTOR_COPY:
                 nc.vector.tensor_copy(out=dst, in_=src)
             else:
                 nc.scalar.copy(out=dst, in_=src)
             return grouped
 
-        def quantise(j, b, grouped):
-            s, q4 = divmod(b, BANKS)
+        def quantise(j, s, q4, grouped):
             rows = slice(P * j, P * j + P)
             for a in range(2):
                 g = 2 * q4 + a
@@ -125,19 +123,20 @@ def tile_quantumgraphneuralnetwork_pa_kernel(tc, latent_re, latent_im, out):
             nc.vector.tensor_add(out=out_sb[j][:, diag], in0=sq_re[j][:, diag], in1=sq_im[j][:, diag])
             store(j, P * j, P * j + P)
 
-        for j in range(TILES):
+        def t_run(j, s):
             held = None
-            for b in range(2 * BANKS):
-                grouped = transposes(j, b)
-                if b > 0:
-                    quantise(j, b - 1, held)
+            for q4 in range(BANKS):
+                grouped = transposes(j, s, q4)
+                if q4 > 0:
+                    quantise(j, s, q4 - 1, held)
                 held = grouped
-            quantise(j, 2 * BANKS - 1, held)
-            if j > 0:
-                extras(j - 1)
-                finish_diag(j - 1)
+            quantise(j, s, BANKS - 1, held)
+
+        t_run(0, 0)
+        t_run(0, 1)
+        for j in range(TILES):
             off = P * j
-            for g_span, b_span, a_span in PROGRAM[j]:
+            for k, (g_span, b_span, a_span) in enumerate(PROGRAM[j]):
                 acc_g = psum.tile([P, N], F32, tag="acc_g", bufs=2, name="acc_g")
                 passes(acc_g, j, 0, 0, g_span, True, False)
                 if b_span is not None:
@@ -146,6 +145,8 @@ def tile_quantumgraphneuralnetwork_pa_kernel(tc, latent_re, latent_im, out):
                     passes(acc_b, j, 0, 1, b_span, True, True)
                     b_sb = epi.tile([P, N], F32, tag="b_sb", name="b_sb")
                     nc.scalar.copy(out=b_sb[:, 0:wb], in_=acc_b[:, 0:wb])
+                if k == 0 and 0 < j < TILES - 1:
+                    t_run(j + 1, 0)
                 if a_span is not None:
                     acc_a = psum.tile([P, N], F32, tag="acc_a", bufs=1, name="acc_a")
                     passes(acc_a, j, 1, 0, a_span, True, True)
@@ -167,4 +168,9 @@ def tile_quantumgraphneuralnetwork_pa_kernel(tc, latent_re, latent_im, out):
                         out=out_sb[j][:, g_span[0] : c1], in0=sq_re[j][:, g_span[0] : c1], in1=sq_im[j][:, g_span[0] : c1]
                     )
                     store(j, g_span[0], c1)
-        finish_diag(TILES - 1)
+            if j < TILES - 1:
+                if j == 0:
+                    t_run(1, 0)
+                t_run(j + 1, 1)
+                extras(j)
+            finish_diag(j)

@@ -24,6 +24,7 @@ PROGRAM = {
     2: [((0, 256), (0, 256), (0, 256)), ((256, 384), None, (256, 384))],
     3: [((0, 256), (0, 256), (0, 256)), ((256, 384), (256, 384), (256, 512)), ((384, 512), None, None)],
 }
+HEAD_IDLE = 5
 VECTOR_COPY = 1
 
 
@@ -46,6 +47,15 @@ def tile_quantumgraphneuralnetwork_pa_kernel(tc, latent_re, latent_im, out):
         a_diag = [keep.tile([P, P], F32, name="a_diag%d" % j) for j in range(TILES)]
         ident = keep.tile([P, P], F32, name="ident")
         warm = keep.tile([P, 2], F32, name="warm")
+        zeros = keep.tile([P, N], BF16, name="zeros")
+        idle_acc = psum.tile([P, N], F32, tag="acc_b", bufs=1, name="idle_acc")
+
+        def idle_matmul():
+            nc.tensor.matmul(out=idle_acc[:], lhsT=zeros[:, 0:P], rhs=zeros[:], start=True, stop=True)
+
+        nc.vector.memset(zeros[:], 0.0)
+        for i in range(HEAD_IDLE):
+            idle_matmul()
 
         for s in range(2):
             for c in range(4):
@@ -65,6 +75,8 @@ def tile_quantumgraphneuralnetwork_pa_kernel(tc, latent_re, latent_im, out):
             for q in range(4):
                 w0 = 512 * q4 + P * q
                 nc.tensor.transpose(tp[:, q, :], words[:, w0 : w0 + P], ident[:])
+            if j == 0:
+                idle_matmul()
             grouped = stage.tile([P, 1024], BF16, tag="grouped", name="grouped", align_bytes=64)
             dst = grouped[:].bitcast(F32).rearrange("p (a n u) -> p a n u", a=2, u=2)
             src = tp[:].rearrange("p (a u) n -> p a n u", u=2)

@@ -24,7 +24,6 @@ PROGRAM = {
     2: [((0, 256), (0, 256), (0, 256)), ((256, 384), None, (256, 384))],
     3: [((0, 256), (0, 256), (0, 256)), ((256, 384), (256, 384), (256, 512)), ((384, 512), None, None)],
 }
-HEAD_IDLE = 5
 VECTOR_COPY = 1
 
 
@@ -47,15 +46,6 @@ def tile_quantumgraphneuralnetwork_pa_kernel(tc, latent_re, latent_im, out):
         a_diag = [keep.tile([P, P], F32, name="a_diag%d" % j) for j in range(TILES)]
         ident = keep.tile([P, P], F32, name="ident")
         warm = keep.tile([P, 2], F32, name="warm")
-        zeros = keep.tile([P, N], BF16, name="zeros")
-        idle_acc = psum.tile([P, N], F32, tag="acc_b", bufs=1, name="idle_acc")
-
-        def idle_matmul():
-            nc.tensor.matmul(out=idle_acc[:], lhsT=zeros[:, 0:P], rhs=zeros[:], start=True, stop=True)
-
-        nc.vector.memset(zeros[:], 0.0)
-        for i in range(HEAD_IDLE):
-            idle_matmul()
 
         for s in range(2):
             for c in range(4):
@@ -75,8 +65,6 @@ def tile_quantumgraphneuralnetwork_pa_kernel(tc, latent_re, latent_im, out):
             for q in range(4):
                 w0 = 512 * q4 + P * q
                 nc.tensor.transpose(tp[:, q, :], words[:, w0 : w0 + P], ident[:])
-            if j == 0:
-                idle_matmul()
             grouped = stage.tile([P, 1024], BF16, tag="grouped", name="grouped", align_bytes=64)
             dst = grouped[:].bitcast(F32).rearrange("p (a n u) -> p a n u", a=2, u=2)
             src = tp[:].rearrange("p (a u) n -> p a n u", u=2)
@@ -157,8 +145,6 @@ def tile_quantumgraphneuralnetwork_pa_kernel(tc, latent_re, latent_im, out):
                     passes(acc_b, j, 0, 1, b_span, True, True)
                     b_sb = epi.tile([P, N], F32, tag="b_sb", name="b_sb")
                     nc.scalar.copy(out=b_sb[:, 0:wb], in_=acc_b[:, 0:wb])
-                if k == 0 and 0 < j < TILES - 1:
-                    t_run(j + 1, 0)
                 if a_span is not None:
                     acc_a = psum.tile([P, N], F32, tag="acc_a", bufs=1, name="acc_a")
                     passes(acc_a, j, 1, 0, a_span, True, True)
@@ -168,6 +154,8 @@ def tile_quantumgraphneuralnetwork_pa_kernel(tc, latent_re, latent_im, out):
                         nc.scalar.activation(out=sq_im[j][:, b_span[0] : b_span[1]], in_=diff[:, 0:wb], func=SQUARE)
                     if a_span[1] > off:
                         nc.vector.tensor_copy(out=a_diag[j][:], in_=acc_a[:, off - a_span[0] : off - a_span[0] + P])
+                if k == 0 and j < TILES - 1:
+                    t_run(j + 1, 0)
                 if j == TILES - 1 and g_span[0] == off:
                     extras(j)
                 passes(acc_g, j, 1, 1, g_span, False, True)
@@ -181,8 +169,6 @@ def tile_quantumgraphneuralnetwork_pa_kernel(tc, latent_re, latent_im, out):
                     )
                     store(j, g_span[0], c1)
             if j < TILES - 1:
-                if j == 0:
-                    t_run(1, 0)
                 t_run(j + 1, 1)
                 extras(j)
             finish_diag(j)

@@ -24,6 +24,7 @@ PROGRAM = {
     2: [((0, 256), (0, 256), (0, 256)), ((256, 384), None, (256, 384))],
     3: [((0, 256), (0, 256), (0, 256)), ((256, 384), (256, 384), (256, 512)), ((384, 512), None, None)],
 }
+HEAD_IDLE = 10
 VECTOR_COPY = 1
 
 
@@ -46,12 +47,22 @@ def tile_quantumgraphneuralnetwork_pa_kernel(tc, latent_re, latent_im, out):
         a_diag = [keep.tile([P, P], F32, name="a_diag%d" % j) for j in range(TILES)]
         ident = keep.tile([P, P], F32, name="ident")
         warm = keep.tile([P, 2], F32, name="warm")
+        zeros = keep.tile([P, N], BF16, name="zeros")
+        idle_acc = psum.tile([P, N], F32, tag="acc_b", bufs=1, name="idle_acc")
+
+        nc.vector.memset(zeros[:], 0.0)
+        for i in range(HEAD_IDLE):
+            nc.tensor.matmul(out=idle_acc[:], lhsT=zeros[:, 0:P], rhs=zeros[:], start=True, stop=True)
 
         for s in range(2):
             for c in range(4):
                 cols = slice(1024 * c, 1024 * c + 1024)
                 nc.sync.dma_start(out=x_sb[s][0][:, cols], in_=latent[s][0:P, cols])
-        for j in range(1, TILES):
+        for s in range(2):
+            for c in range(2):
+                cols = slice(2048 * c, 2048 * c + 2048)
+                nc.sync.dma_start(out=x_sb[s][1][:, cols], in_=latent[s][P : 2 * P, cols])
+        for j in range(2, TILES):
             for s in range(2):
                 nc.sync.dma_start(out=x_sb[s][j][:], in_=latent[s][P * j : P * j + P, :])
 

@@ -24,7 +24,7 @@ PROGRAM = {
     2: [((0, 256), (0, 256), (0, 256)), ((256, 384), None, (256, 384))],
     3: [((0, 256), (0, 256), (0, 256)), ((256, 384), (256, 384), (256, 512)), ((384, 512), None, None)],
 }
-HEAD_IDLE = 10
+HEAD_IDLE = 4
 VECTOR_COPY = 1
 
 
@@ -54,14 +54,11 @@ def tile_quantumgraphneuralnetwork_pa_kernel(tc, latent_re, latent_im, out):
         for i in range(HEAD_IDLE):
             nc.tensor.matmul(out=idle_acc[:], lhsT=zeros[:, 0:P], rhs=zeros[:], start=True, stop=True)
 
-        for s in range(2):
-            for c in range(4):
-                cols = slice(1024 * c, 1024 * c + 1024)
-                nc.sync.dma_start(out=x_sb[s][0][:, cols], in_=latent[s][0:P, cols])
-        for s in range(2):
-            for c in range(2):
-                cols = slice(2048 * c, 2048 * c + 2048)
-                nc.sync.dma_start(out=x_sb[s][1][:, cols], in_=latent[s][P : 2 * P, cols])
+        for c in range(4):
+            cols = slice(1024 * c, 1024 * c + 1024)
+            for s in range(2):
+                for j in range(2):
+                    nc.sync.dma_start(out=x_sb[s][j][:, cols], in_=latent[s][P * j : P * j + P, cols])
         for j in range(2, TILES):
             for s in range(2):
                 nc.sync.dma_start(out=x_sb[s][j][:], in_=latent[s][P * j : P * j + P, :])
@@ -70,7 +67,7 @@ def tile_quantumgraphneuralnetwork_pa_kernel(tc, latent_re, latent_im, out):
         nc.vector.memset(warm[:, 0:1], 0.0)
         nc.scalar.activation(out=warm[:, 1:2], in_=warm[:, 0:1], func=SQUARE)
 
-        def transposes(j, s, q4):
+        def transposes(j, s, q4, vector):
             words = x_sb[s][j][:].bitcast(F32)
             tp = psum.tile([P, 4, P], F32, tag="tp", bufs=4, name="tp")
             for q in range(4):
@@ -79,7 +76,7 @@ def tile_quantumgraphneuralnetwork_pa_kernel(tc, latent_re, latent_im, out):
             grouped = stage.tile([P, 1024], BF16, tag="grouped", name="grouped", align_bytes=64)
             dst = grouped[:].bitcast(F32).rearrange("p (a n u) -> p a n u", a=2, u=2)
             src = tp[:].rearrange("p (a u) n -> p a n u", u=2)
-            if q4 == VECTOR_COPY:
+            if vector:
                 nc.vector.tensor_copy(out=dst, in_=src)
             else:
                 nc.scalar.copy(out=dst, in_=src)
@@ -95,10 +92,10 @@ def tile_quantumgraphneuralnetwork_pa_kernel(tc, latent_re, latent_im, out):
                     in_=grouped[:, 512 * a : 512 * a + 512],
                 )
 
-        def passes(acc, j, stat, mov, span, first, last):
+        def passes(acc, j, stat, mov, span, first, last, gs=range(PASSES)):
             rows = slice(P * j, P * j + P)
             cols = slice(span[0], span[1])
-            for g in range(PASSES):
+            for g in gs:
                 nc.tensor.matmul_mx(
                     out=acc[:, 0 : span[1] - span[0]],
                     lhsT=codes[stat][:, g, rows].bitcast(FP8X4),
@@ -129,6 +126,20 @@ def tile_quantumgraphneuralnetwork_pa_kernel(tc, latent_re, latent_im, out):
                     in_=m_sb[:, 0:j, :],
                 )
 
+        def extras_pair():
+            ex = psum.tile([P, 4, P], F32, tag="acc_g", bufs=2, name="ex")
+            for j in range(2):
+                nc.tensor.transpose(ex[:, j, :], a_diag[j][:], ident[:])
+            nc.tensor.transpose(ex[:, 2, :], out_sb[1][:, 0:P], ident[:])
+            for j in range(2):
+                diag = slice(P * j, P * j + P)
+                diff = epi.tile([P, P], F32, tag="diff_d", name="diff_d")
+                nc.vector.tensor_sub(out=diff[:], in0=a_diag[j][:], in1=ex[:, j, :])
+                nc.vector.tensor_mul(out=sq_im[j][:, diag], in0=diff[:], in1=diff[:])
+            m_sb = epi.tile([P, 3, P], F32, tag="m_sb", name="m_sb")
+            nc.scalar.copy(out=m_sb[:, 0, :], in_=ex[:, 2, :])
+            nc.sync.dma_start(out=out[0:P, P : 2 * P], in_=m_sb[:, 0, :])
+
         def finish_diag(j):
             diag = slice(P * j, P * j + P)
             nc.vector.tensor_add(out=out_sb[j][:, diag], in0=sq_re[j][:, diag], in1=sq_im[j][:, diag])
@@ -137,15 +148,59 @@ def tile_quantumgraphneuralnetwork_pa_kernel(tc, latent_re, latent_im, out):
         def t_run(j, s):
             held = None
             for q4 in range(BANKS):
-                grouped = transposes(j, s, q4)
+                grouped = transposes(j, s, q4, q4 == VECTOR_COPY)
                 if q4 > 0:
                     quantise(j, s, q4 - 1, held)
                 held = grouped
             quantise(j, s, BANKS - 1, held)
 
-        t_run(0, 0)
-        t_run(0, 1)
-        for j in range(TILES):
+        def t_pair(q4, s):
+            held = [transposes(j, s, q4, False) for j in range(2)]
+            for j in range(2):
+                quantise(j, s, q4, held[j])
+
+        acc_g1 = psum.tile([P, N], F32, tag="acc_g", bufs=2, name="acc_g1")
+        acc_g0 = psum.tile([P, N], F32, tag="acc_g", bufs=2, name="acc_g0")
+        acc_a1 = psum.tile([P, N], F32, tag="acc_a", bufs=1, name="acc_a1")
+        accs = {}
+
+        def m_pair(q4):
+            if q4 == 0:
+                accs["b"] = psum.tile([P, N], F32, tag="acc_b", bufs=1, name="acc_b1")
+            gs = range(2 * q4, 2 * q4 + 2)
+            passes(acc_g1, 1, 0, 0, (0, 256), True, False, gs)
+            passes(acc_g0, 0, 0, 0, (0, 128), True, False, gs)
+            passes(accs["b"], 1, 0, 1, (0, 128), True, True, gs)
+            passes(acc_a1, 1, 1, 0, (0, 256), True, True, gs)
+            passes(acc_g1, 1, 1, 1, (0, 256), False, True, gs)
+            passes(acc_g0, 0, 1, 1, (0, 128), False, True, gs)
+
+        t_pair(0, 0)
+        t_pair(0, 1)
+        for q4 in range(1, BANKS):
+            t_pair(q4, 0)
+            t_pair(q4, 1)
+            m_pair(q4 - 1)
+        t_run(2, 0)
+        m_pair(BANKS - 1)
+        b_sb = epi.tile([P, N], F32, tag="b_sb", name="b_sb")
+        nc.scalar.copy(out=b_sb[:, 0:P], in_=accs["b"][:, 0:P])
+        acc_a0 = psum.tile([P, N], F32, tag="acc_b", bufs=1, name="acc_a0")
+        passes(acc_a0, 0, 1, 0, (0, 128), True, True)
+        nc.scalar.activation(out=sq_re[1][:, 0:256], in_=acc_g1[:, 0:256], func=SQUARE)
+        nc.scalar.activation(out=sq_re[0][:, 0:P], in_=acc_g0[:, 0:P], func=SQUARE)
+        diff = epi.tile([P, N], F32, tag="diff", name="diff")
+        nc.vector.tensor_sub(out=diff[:, 0:P], in0=acc_a1[:, 0:P], in1=b_sb[:, 0:P])
+        nc.vector.tensor_copy(out=a_diag[1][:], in_=acc_a1[:, P : 2 * P])
+        nc.vector.tensor_copy(out=a_diag[0][:], in_=acc_a0[:, 0:P])
+        nc.scalar.activation(out=sq_im[1][:, 0:P], in_=diff[:, 0:P], func=SQUARE)
+        nc.vector.tensor_add(out=out_sb[1][:, 0:P], in0=sq_re[1][:, 0:P], in1=sq_im[1][:, 0:P])
+        store(1, 0, P)
+        t_run(2, 1)
+        extras_pair()
+        finish_diag(0)
+        finish_diag(1)
+        for j in range(2, TILES):
             off = P * j
             for k, (g_span, b_span, a_span) in enumerate(PROGRAM[j]):
                 acc_g = psum.tile([P, N], F32, tag="acc_g", bufs=2, name="acc_g")

@@ -15,17 +15,13 @@ N = 512
 D = 4096
 TILES = N // P
 PASSES = D // 512
-BANKS = 4
+CHUNKS = 4
 FLOPS = 4 * 2 * N * N * D
+RE, IM = 0, 1
 
-PROGRAM = {
-    0: [((0, 128), None, (0, 128))],
-    1: [((0, 256), (0, 128), (0, 256))],
-    2: [((0, 256), (0, 256), (0, 256)), ((256, 384), None, (256, 384))],
-    3: [((0, 256), (0, 256), (0, 256)), ((256, 384), (256, 384), (256, 512)), ((384, 512), None, None)],
-}
 HEAD_IDLE = 4
 VECTOR_COPY = 1
+LOADS = ((0, 1024), (1024, 2048), (2048, 3072), (3072, 4096))
 
 
 def tile_quantumgraphneuralnetwork_pa_kernel(tc, latent_re, latent_im, out):
@@ -44,34 +40,38 @@ def tile_quantumgraphneuralnetwork_pa_kernel(tc, latent_re, latent_im, out):
         out_sb = [keep.tile([P, N], F32, name="out_sb%d" % j) for j in range(TILES)]
         sq_re = [keep.tile([P, N], F32, name="sq_re%d" % j) for j in range(TILES)]
         sq_im = [keep.tile([P, N], F32, name="sq_im%d" % j) for j in range(TILES)]
-        a_diag = [keep.tile([P, P], F32, name="a_diag%d" % j) for j in range(TILES)]
+        a_sb = [keep.tile([P, 2 * P], F32, name="a_sb%d" % j) for j in range(TILES)]
         ident = keep.tile([P, P], F32, name="ident")
         warm = keep.tile([P, 2], F32, name="warm")
         zeros = keep.tile([P, N], BF16, name="zeros")
-        idle_acc = psum.tile([P, N], F32, tag="acc_b", bufs=1, name="idle_acc")
+        idle_acc = psum.tile([P, 4, P], F32, tag="tp", bufs=4, name="idle_acc")
 
         nc.vector.memset(zeros[:], 0.0)
         for i in range(HEAD_IDLE):
-            nc.tensor.matmul(out=idle_acc[:], lhsT=zeros[:, 0:P], rhs=zeros[:], start=True, stop=True)
+            nc.tensor.matmul(out=idle_acc[:].rearrange("p e n -> p (e n)"), lhsT=zeros[:, 0:P], rhs=zeros[:], start=True, stop=True)
 
-        for c in range(4):
-            cols = slice(1024 * c, 1024 * c + 1024)
+        def load(s, j, c0, c1):
+            nc.sync.dma_start(out=x_sb[s][j][:, c0:c1], in_=latent[s][P * j : P * j + P, c0:c1])
+
+        for c0, c1 in LOADS:
             for s in range(2):
                 for j in range(2):
-                    nc.sync.dma_start(out=x_sb[s][j][:, cols], in_=latent[s][P * j : P * j + P, cols])
-        for j in range(2, TILES):
-            for s in range(2):
-                nc.sync.dma_start(out=x_sb[s][j][:], in_=latent[s][P * j : P * j + P, :])
+                    load(s, j, c0, c1)
+        load(RE, 2, 0, D // 2)
+        load(RE, 2, D // 2, D)
+        load(IM, 2, 0, D)
+        load(RE, 3, 0, D)
+        load(IM, 3, 0, D)
 
         make_identity(nc, ident[:])
         nc.vector.memset(warm[:, 0:1], 0.0)
         nc.scalar.activation(out=warm[:, 1:2], in_=warm[:, 0:1], func=SQUARE)
 
-        def transposes(j, s, q4, vector):
+        def transposes(j, s, c, vector):
             words = x_sb[s][j][:].bitcast(F32)
             tp = psum.tile([P, 4, P], F32, tag="tp", bufs=4, name="tp")
             for q in range(4):
-                w0 = 512 * q4 + P * q
+                w0 = 512 * c + P * q
                 nc.tensor.transpose(tp[:, q, :], words[:, w0 : w0 + P], ident[:])
             grouped = stage.tile([P, 1024], BF16, tag="grouped", name="grouped", align_bytes=64)
             dst = grouped[:].bitcast(F32).rearrange("p (a n u) -> p a n u", a=2, u=2)
@@ -82,15 +82,24 @@ def tile_quantumgraphneuralnetwork_pa_kernel(tc, latent_re, latent_im, out):
                 nc.scalar.copy(out=dst, in_=src)
             return grouped
 
-        def quantise(j, s, q4, grouped):
+        def quantise(j, s, c, grouped):
             rows = slice(P * j, P * j + P)
             for a in range(2):
-                g = 2 * q4 + a
+                g = 2 * c + a
                 nc.vector.quantize_mx(
                     out=codes[s][:, g, rows].bitcast(FP8X4),
                     scales=scales[s][:, g, rows],
                     in_=grouped[:, 512 * a : 512 * a + 512],
                 )
+
+        def t_banks(*banks):
+            held = None
+            for i, bank in enumerate(banks):
+                grouped = transposes(*bank, i % 3 == VECTOR_COPY)
+                if held is not None:
+                    quantise(*banks[i - 1], held)
+                held = grouped
+            quantise(*banks[-1], held)
 
         def passes(acc, j, stat, mov, span, first, last, gs=range(PASSES)):
             rows = slice(P * j, P * j + P)
@@ -106,135 +115,156 @@ def tile_quantumgraphneuralnetwork_pa_kernel(tc, latent_re, latent_im, out):
                     stop=(last and g == PASSES - 1),
                 )
 
+        def bank():
+            return psum.tile([P, N], F32, tag="acc", bufs=4, name="acc")
+
+        def ex_bank():
+            return psum.tile([P, 4, P], F32, tag="tp", bufs=4, name="ex")
+
         def store(j, c0, c1):
             nc.sync.dma_start(out=out[P * j : P * j + P, c0:c1], in_=out_sb[j][:, c0:c1])
 
-        def extras(j):
-            ex = psum.tile([P, 4, P], F32, tag="acc_g", bufs=2, name="ex")
-            nc.tensor.transpose(ex[:, 0, :], a_diag[j][:], ident[:])
-            for i in range(j):
-                nc.tensor.transpose(ex[:, 1 + i, :], out_sb[j][:, P * i : P * i + P], ident[:])
-            diag = slice(P * j, P * j + P)
-            diff = epi.tile([P, P], F32, tag="diff_d", name="diff_d")
-            nc.vector.tensor_sub(out=diff[:], in0=a_diag[j][:], in1=ex[:, 0, :])
-            nc.vector.tensor_mul(out=sq_im[j][:, diag], in0=diff[:], in1=diff[:])
-            if j > 0:
-                m_sb = epi.tile([P, 3, P], F32, tag="m_sb", name="m_sb")
-                nc.scalar.copy(out=m_sb[:, 0:j, :], in_=ex[:, 1 : 1 + j, :])
-                nc.sync.dma_start(
-                    out=out[0 : P * j, diag].rearrange("(i p) c -> p i c", p=P),
-                    in_=m_sb[:, 0:j, :],
-                )
+        def finish(j, c0, c1):
+            nc.vector.tensor_add(out=out_sb[j][:, c0:c1], in0=sq_re[j][:, c0:c1], in1=sq_im[j][:, c0:c1])
+            store(j, c0, c1)
 
-        def extras_pair():
-            ex = psum.tile([P, 4, P], F32, tag="acc_g", bufs=2, name="ex")
-            for j in range(2):
-                nc.tensor.transpose(ex[:, j, :], a_diag[j][:], ident[:])
-            nc.tensor.transpose(ex[:, 2, :], out_sb[1][:, 0:P], ident[:])
-            for j in range(2):
-                diag = slice(P * j, P * j + P)
-                diff = epi.tile([P, P], F32, tag="diff_d", name="diff_d")
-                nc.vector.tensor_sub(out=diff[:], in0=a_diag[j][:], in1=ex[:, j, :])
-                nc.vector.tensor_mul(out=sq_im[j][:, diag], in0=diff[:], in1=diff[:])
-            m_sb = epi.tile([P, 3, P], F32, tag="m_sb", name="m_sb")
-            nc.scalar.copy(out=m_sb[:, 0, :], in_=ex[:, 2, :])
-            nc.sync.dma_start(out=out[0:P, P : 2 * P], in_=m_sb[:, 0, :])
+        def mirror_turn(ex, places):
+            for e, (j, i) in places:
+                nc.tensor.transpose(ex[:, e, :], out_sb[j][:, P * i : P * i + P], ident[:])
 
-        def finish_diag(j):
-            diag = slice(P * j, P * j + P)
-            nc.vector.tensor_add(out=out_sb[j][:, diag], in0=sq_re[j][:, diag], in1=sq_im[j][:, diag])
-            store(j, P * j, P * j + P)
+        def mirror_store(ex, e0, i0, n, j):
+            m_sb = epi.tile([P, 2, P], F32, tag="m_sb", bufs=4, name="m_sb")
+            nc.scalar.copy(out=m_sb[:, 0:n, :], in_=ex[:, e0 : e0 + n, :])
+            nc.sync.dma_start(
+                out=out[P * i0 : P * (i0 + n), P * j : P * j + P].rearrange("(i p) c -> p i c", p=P),
+                in_=m_sb[:, 0:n, :],
+            )
 
-        def t_run(j, s):
-            held = None
-            for q4 in range(BANKS):
-                grouped = transposes(j, s, q4, q4 == VECTOR_COPY)
-                if q4 > 0:
-                    quantise(j, s, q4 - 1, held)
-                held = grouped
-            quantise(j, s, BANKS - 1, held)
+        def a_turn(ex, j):
+            nc.tensor.transpose(ex[:, 0, :], a_sb[j][:, P : 2 * P], ident[:])
+            nc.tensor.transpose(ex[:, 1, :], a_sb[j + 1][:, P : 2 * P], ident[:])
+            nc.tensor.transpose(ex[:, 2, :], a_sb[j][:, 0:P], ident[:])
 
-        def t_pair(q4, s):
-            held = [transposes(j, s, q4, False) for j in range(2)]
-            for j in range(2):
-                quantise(j, s, q4, held[j])
+        def a_square(ex, j):
+            lo, mid, hi = P * j, P * j + P, P * j + 2 * P
+            diff = epi.tile([P, 2, P], F32, tag="diff_pair", name="diff_pair")
+            nc.vector.tensor_sub(
+                out=diff[:], in0=a_sb[j + 1][:].rearrange("p (e n) -> p e n", e=2), in1=ex[:, 0:2, :]
+            )
+            diff_d = epi.tile([P, P], F32, tag="diff_d", name="diff_d")
+            nc.vector.tensor_sub(out=diff_d[:], in0=a_sb[j][:, 0:P], in1=ex[:, 2, :])
+            nc.scalar.activation(
+                out=sq_im[j + 1][:, lo:hi].rearrange("p (e n) -> p e n", e=2), in_=diff[:], func=SQUARE
+            )
+            nc.vector.tensor_mul(out=sq_im[j][:, lo:mid], in0=diff_d[:], in1=diff_d[:])
 
-        acc_g1 = psum.tile([P, N], F32, tag="acc_g", bufs=2, name="acc_g1")
-        acc_g0 = psum.tile([P, N], F32, tag="acc_g", bufs=2, name="acc_g0")
-        acc_a1 = psum.tile([P, N], F32, tag="acc_a", bufs=1, name="acc_a1")
-        accs = {}
+        a0, a1, g1, g0 = bank(), bank(), bank(), bank()
 
-        def m_pair(q4):
-            if q4 == 0:
-                accs["b"] = psum.tile([P, N], F32, tag="acc_b", bufs=1, name="acc_b1")
-            gs = range(2 * q4, 2 * q4 + 2)
-            passes(acc_g1, 1, 0, 0, (0, 256), True, False, gs)
-            passes(acc_g0, 0, 0, 0, (0, 128), True, False, gs)
-            passes(accs["b"], 1, 0, 1, (0, 128), True, True, gs)
-            passes(acc_a1, 1, 1, 0, (0, 256), True, True, gs)
-            passes(acc_g1, 1, 1, 1, (0, 256), False, True, gs)
-            passes(acc_g0, 0, 1, 1, (0, 128), False, True, gs)
+        def pair_im(c):
+            gs = range(2 * c, 2 * c + 2)
+            passes(g1, 1, IM, IM, (0, 256), False, True, gs)
+            passes(g0, 0, IM, IM, (0, 128), False, True, gs)
 
-        t_pair(0, 0)
-        t_pair(0, 1)
-        for q4 in range(1, BANKS):
-            t_pair(q4, 0)
-            t_pair(q4, 1)
-            m_pair(q4 - 1)
-        t_run(2, 0)
-        m_pair(BANKS - 1)
-        b_sb = epi.tile([P, N], F32, tag="b_sb", name="b_sb")
-        nc.scalar.copy(out=b_sb[:, 0:P], in_=accs["b"][:, 0:P])
-        acc_a0 = psum.tile([P, N], F32, tag="acc_b", bufs=1, name="acc_a0")
-        passes(acc_a0, 0, 1, 0, (0, 128), True, True)
-        nc.scalar.activation(out=sq_re[1][:, 0:256], in_=acc_g1[:, 0:256], func=SQUARE)
-        nc.scalar.activation(out=sq_re[0][:, 0:P], in_=acc_g0[:, 0:P], func=SQUARE)
-        diff = epi.tile([P, N], F32, tag="diff", name="diff")
-        nc.vector.tensor_sub(out=diff[:, 0:P], in0=acc_a1[:, 0:P], in1=b_sb[:, 0:P])
-        nc.vector.tensor_copy(out=a_diag[1][:], in_=acc_a1[:, P : 2 * P])
-        nc.vector.tensor_copy(out=a_diag[0][:], in_=acc_a0[:, 0:P])
-        nc.scalar.activation(out=sq_im[1][:, 0:P], in_=diff[:, 0:P], func=SQUARE)
-        nc.vector.tensor_add(out=out_sb[1][:, 0:P], in0=sq_re[1][:, 0:P], in1=sq_im[1][:, 0:P])
-        store(1, 0, P)
-        t_run(2, 1)
-        extras_pair()
-        finish_diag(0)
-        finish_diag(1)
-        for j in range(2, TILES):
-            off = P * j
-            for k, (g_span, b_span, a_span) in enumerate(PROGRAM[j]):
-                acc_g = psum.tile([P, N], F32, tag="acc_g", bufs=2, name="acc_g")
-                passes(acc_g, j, 0, 0, g_span, True, False)
-                if b_span is not None:
-                    wb = b_span[1] - b_span[0]
-                    acc_b = psum.tile([P, N], F32, tag="acc_b", bufs=1, name="acc_b")
-                    passes(acc_b, j, 0, 1, b_span, True, True)
-                    b_sb = epi.tile([P, N], F32, tag="b_sb", name="b_sb")
-                    nc.scalar.copy(out=b_sb[:, 0:wb], in_=acc_b[:, 0:wb])
-                if a_span is not None:
-                    acc_a = psum.tile([P, N], F32, tag="acc_a", bufs=1, name="acc_a")
-                    passes(acc_a, j, 1, 0, a_span, True, True)
-                    if b_span is not None:
-                        diff = epi.tile([P, N], F32, tag="diff", name="diff")
-                        nc.vector.tensor_sub(out=diff[:, 0:wb], in0=acc_a[:, 0:wb], in1=b_sb[:, 0:wb])
-                        nc.scalar.activation(out=sq_im[j][:, b_span[0] : b_span[1]], in_=diff[:, 0:wb], func=SQUARE)
-                    if a_span[1] > off:
-                        nc.vector.tensor_copy(out=a_diag[j][:], in_=acc_a[:, off - a_span[0] : off - a_span[0] + P])
-                if k == 0 and j < TILES - 1:
-                    t_run(j + 1, 0)
-                if j == TILES - 1 and g_span[0] == off:
-                    extras(j)
-                passes(acc_g, j, 1, 1, g_span, False, True)
-                nc.scalar.activation(
-                    out=sq_re[j][:, g_span[0] : g_span[1]], in_=acc_g[:, 0 : g_span[1] - g_span[0]], func=SQUARE
-                )
-                c1 = min(g_span[1], off)
-                if c1 > g_span[0]:
-                    nc.vector.tensor_add(
-                        out=out_sb[j][:, g_span[0] : c1], in0=sq_re[j][:, g_span[0] : c1], in1=sq_im[j][:, g_span[0] : c1]
-                    )
-                    store(j, g_span[0], c1)
-            if j < TILES - 1:
-                t_run(j + 1, 1)
-                extras(j)
-            finish_diag(j)
+        def pair_rest(c):
+            gs = range(2 * c, 2 * c + 2)
+            passes(g1, 1, RE, RE, (0, 256), True, False, gs)
+            passes(g0, 0, RE, RE, (0, 128), True, False, gs)
+            passes(a1, 1, IM, RE, (0, 256), True, True, gs)
+            passes(a0, 0, IM, RE, (0, 256), True, True, gs)
+
+        t_banks((0, RE, 0), (1, RE, 0))
+        t_banks((0, IM, 0), (1, IM, 0))
+        t_banks((0, RE, 1), (1, RE, 1))
+        pair_rest(0)
+        t_banks((0, IM, 1), (1, IM, 1), (0, RE, 2), (1, RE, 2))
+        pair_im(0)
+        pair_rest(1)
+        t_banks((0, IM, 2), (1, IM, 2), (0, RE, 3), (1, RE, 3))
+        pair_im(1)
+        pair_rest(2)
+        t_banks((0, IM, 3), (1, IM, 3), (2, RE, 0), (2, RE, 1))
+        pair_im(2)
+        pair_rest(3)
+        pair_im(3)
+        nc.vector.tensor_copy(out=a_sb[0][:], in_=a0[:, 0:256])
+        nc.scalar.copy(out=a_sb[1][:], in_=a1[:, 0:256])
+        t_banks((2, RE, 2), (2, RE, 3), (2, IM, 0), (2, IM, 1), (2, IM, 2))
+        nc.scalar.activation(out=sq_re[1][:, 0:256], in_=g1[:, 0:256], func=SQUARE)
+        nc.scalar.activation(out=sq_re[0][:, 0:128], in_=g0[:, 0:128], func=SQUARE)
+
+        far = (0, 2 * P)
+
+        def copy_b(acc_b):
+            b_sb = epi.tile([P, 2 * P], F32, tag="b_sb", name="b_sb")
+            nc.scalar.copy(out=b_sb[:], in_=acc_b[:, 0:256])
+            return b_sb
+
+        def far_sub(j, acc_a, b_sb):
+            diff = epi.tile([P, 2 * P], F32, tag="diff", name="diff")
+            nc.vector.tensor_sub(out=diff[:], in0=acc_a[:, 0:256], in1=b_sb[:])
+            nc.scalar.activation(out=sq_im[j][:, 0:256], in_=diff[:], func=SQUARE)
+
+        g2 = bank()
+        passes(g2, 2, RE, RE, far, True, False)
+        acc_b = bank()
+        passes(acc_b, 2, RE, IM, far, True, True, range(0, 6))
+        t_banks((2, IM, 3), (3, RE, 0), (3, RE, 1), (3, RE, 2), (3, RE, 3))
+        ex = ex_bank()
+        a_turn(ex, 0)
+        passes(acc_b, 2, RE, IM, far, True, True, range(6, 8))
+        b_sb = copy_b(acc_b)
+        a_square(ex, 0)
+        finish(1, 0, 256)
+        finish(0, 0, 128)
+        acc_a = bank()
+        passes(acc_a, 2, IM, RE, far, True, True)
+        far_sub(2, acc_a, b_sb)
+        passes(g2, 2, IM, IM, far, False, True)
+        nc.scalar.activation(out=sq_re[2][:, 0:256], in_=g2[:, 0:256], func=SQUARE)
+        t_banks((3, IM, 0), (3, IM, 1), (3, IM, 2), (3, IM, 3))
+        finish(2, 0, 256)
+        g3 = bank()
+        passes(g3, 3, RE, RE, far, True, False)
+        acc_b = bank()
+        passes(acc_b, 3, RE, IM, far, True, True)
+        b_sb = copy_b(acc_b)
+        acc_a = bank()
+        passes(acc_a, 3, IM, RE, far, True, True)
+        far_sub(3, acc_a, b_sb)
+        passes(g3, 3, IM, IM, far, False, True)
+        nc.scalar.activation(out=sq_re[3][:, 0:256], in_=g3[:, 0:256], func=SQUARE)
+        finish(3, 0, 256)
+
+        near = (2 * P, 4 * P)
+        a2 = bank()
+        passes(a2, 2, IM, RE, near, True, True)
+        nc.vector.tensor_copy(out=a_sb[2][:], in_=a2[:, 0:256])
+        a3 = bank()
+        passes(a3, 3, IM, RE, near, True, True)
+        nc.scalar.copy(out=a_sb[3][:], in_=a3[:, 0:256])
+        g3 = bank()
+        passes(g3, 3, RE, RE, near, True, False)
+        ex_m = ex_bank()
+        mirror_turn(ex_m, [(0, (2, 0)), (1, (2, 1)), (2, (3, 0)), (3, (3, 1))])
+        ex = ex_bank()
+        a_turn(ex, 2)
+        mirror_turn(ex, [(3, (1, 0))])
+        mirror_store(ex_m, 0, 0, 2, 2)
+        mirror_store(ex_m, 2, 0, 2, 3)
+        a_square(ex, 2)
+        mirror_store(ex, 3, 0, 1, 1)
+        passes(g3, 3, IM, IM, near, False, True)
+        nc.scalar.activation(out=sq_re[3][:, 256:384], in_=g3[:, 0:128], func=SQUARE)
+        nc.vector.tensor_add(out=out_sb[3][:, 256:384], in0=sq_re[3][:, 256:384], in1=sq_im[3][:, 256:384])
+        nc.scalar.activation(out=sq_re[3][:, 384:512], in_=g3[:, 128:256], func=SQUARE)
+        nc.vector.tensor_add(out=out_sb[3][:, 384:512], in0=sq_re[3][:, 384:512], in1=sq_im[3][:, 384:512])
+        store(3, 256, 512)
+        g2 = bank()
+        diag = (2 * P, 3 * P)
+        passes(g2, 2, RE, RE, diag, True, False)
+        passes(g2, 2, IM, IM, diag, False, True)
+        ex_m = ex_bank()
+        mirror_turn(ex_m, [(0, (3, 2))])
+        nc.scalar.activation(out=sq_re[2][:, 256:384], in_=g2[:, 0:128], func=SQUARE)
+        finish(2, 256, 384)
+        mirror_store(ex_m, 0, 2, 1, 3)

@@ -37,7 +37,7 @@ def tile_quantumgraphneuralnetwork_pa_kernel(tc, latent_re, latent_im, out):
         x_sb = [[keep.tile([P, D], BF16, name="x%d_%d" % (s, j)) for j in range(TILES)] for s in range(2)]
         codes = [keep.tile([P, PASSES, N], U32, name="codes%d" % s, align_bytes=64) for s in range(2)]
         scales = [keep.tile([P, PASSES, N], U8, name="scales%d" % s, align_bytes=64) for s in range(2)]
-        out_sb = [keep.tile([P, N], F32, name="out_sb%d" % j) for j in range(TILES)]
+        out_sb = [keep.tile([P, N], F32, name="out_sb%d" % j, align_bytes=64) for j in range(TILES)]
         sq_re = [keep.tile([P, N], F32, name="sq_re%d" % j) for j in range(TILES)]
         sq_im = [keep.tile([P, N], F32, name="sq_im%d" % j) for j in range(TILES)]
         a_sb = [keep.tile([P, 2 * P], F32, name="a_sb%d" % j) for j in range(TILES)]
@@ -128,17 +128,14 @@ def tile_quantumgraphneuralnetwork_pa_kernel(tc, latent_re, latent_im, out):
             nc.vector.tensor_add(out=out_sb[j][:, c0:c1], in0=sq_re[j][:, c0:c1], in1=sq_im[j][:, c0:c1])
             store(j, c0, c1)
 
-        def mirror_turn(ex, places):
-            for e, (j, i) in places:
-                nc.tensor.transpose(ex[:, e, :], out_sb[j][:, P * i : P * i + P], ident[:])
-
-        def mirror_store(ex, e0, i0, n, j):
-            m_sb = epi.tile([P, 2, P], F32, tag="m_sb", bufs=4, name="m_sb")
-            nc.scalar.copy(out=m_sb[:, 0:n, :], in_=ex[:, e0 : e0 + n, :])
-            nc.sync.dma_start(
-                out=out[P * i0 : P * (i0 + n), P * j : P * j + P].rearrange("(i p) c -> p i c", p=P),
-                in_=m_sb[:, 0:n, :],
-            )
+        def mirror(j, width):
+            turned = epi.tile([P, width], F32, tag="turned%d" % j, bufs=1, name="turned", align_bytes=64)
+            nc.vector.transpose(turned[:], out_sb[j][:, 0:width])
+            for q in range(4):
+                nc.sync.dma_start(
+                    out=out[0:width, P * j + 32 * q : P * j + 32 * q + 32].rearrange("(b c) r -> c b r", c=32),
+                    in_=turned[32 * q : 32 * q + 32, :].rearrange("c (b r) -> c b r", r=32),
+                )
 
         def a_turn(ex, j):
             nc.tensor.transpose(ex[:, 0, :], a_sb[j][:, P : 2 * P], ident[:])
@@ -223,6 +220,8 @@ def tile_quantumgraphneuralnetwork_pa_kernel(tc, latent_re, latent_im, out):
         nc.scalar.activation(out=sq_re[2][:, 0:256], in_=g2[:, 0:256], func=SQUARE)
         t_banks((3, IM, 0), (3, IM, 1), (3, IM, 2), (3, IM, 3))
         finish(2, 0, 256)
+        mirror(1, P)
+        mirror(2, 2 * P)
         g3 = bank()
         passes(g3, 3, RE, RE, far, True, False)
         acc_b = bank()
@@ -234,6 +233,7 @@ def tile_quantumgraphneuralnetwork_pa_kernel(tc, latent_re, latent_im, out):
         passes(g3, 3, IM, IM, far, False, True)
         nc.scalar.activation(out=sq_re[3][:, 0:256], in_=g3[:, 0:256], func=SQUARE)
         finish(3, 0, 256)
+        mirror(3, 2 * P)
 
         near = (2 * P, 4 * P)
         a2 = bank()
@@ -244,15 +244,9 @@ def tile_quantumgraphneuralnetwork_pa_kernel(tc, latent_re, latent_im, out):
         nc.scalar.copy(out=a_sb[3][:], in_=a3[:, 0:256])
         g3 = bank()
         passes(g3, 3, RE, RE, near, True, False)
-        ex_m = ex_bank()
-        mirror_turn(ex_m, [(0, (2, 0)), (1, (2, 1)), (2, (3, 0)), (3, (3, 1))])
         ex = ex_bank()
         a_turn(ex, 2)
-        mirror_turn(ex, [(3, (1, 0))])
-        mirror_store(ex_m, 0, 0, 2, 2)
-        mirror_store(ex_m, 2, 0, 2, 3)
         a_square(ex, 2)
-        mirror_store(ex, 3, 0, 1, 1)
         passes(g3, 3, IM, IM, near, False, True)
         nc.scalar.activation(out=sq_re[3][:, 256:384], in_=g3[:, 0:128], func=SQUARE)
         nc.vector.tensor_add(out=out_sb[3][:, 256:384], in0=sq_re[3][:, 256:384], in1=sq_im[3][:, 256:384])
@@ -263,8 +257,10 @@ def tile_quantumgraphneuralnetwork_pa_kernel(tc, latent_re, latent_im, out):
         diag = (2 * P, 3 * P)
         passes(g2, 2, RE, RE, diag, True, False)
         passes(g2, 2, IM, IM, diag, False, True)
-        ex_m = ex_bank()
-        mirror_turn(ex_m, [(0, (3, 2))])
+        ex = ex_bank()
+        nc.tensor.transpose(ex[:, 0, :], out_sb[3][:, 256:384], ident[:])
         nc.scalar.activation(out=sq_re[2][:, 256:384], in_=g2[:, 0:128], func=SQUARE)
         finish(2, 256, 384)
-        mirror_store(ex_m, 0, 2, 1, 3)
+        m_sb = epi.tile([P, P], F32, tag="m_sb", name="m_sb")
+        nc.scalar.copy(out=m_sb[:], in_=ex[:, 0, :])
+        nc.sync.dma_start(out=out[256:384, 384:512], in_=m_sb[:])

@@ -209,39 +209,35 @@ def tile_quantumgraphneuralnetwork_pa_kernel(tc, latent_re, latent_im, out):
         ex = ex_bank()
         a_turn(ex, 0)
         passes(acc_b, 2, RE, IM, far, True, True, range(6, 8))
-        b_sb = copy_b(acc_b)
+        b2_sb = copy_b(acc_b)
         a_square(ex, 0)
         finish(1, 0, 256)
         finish(0, 0, 128)
-        acc_a = bank()
-        passes(acc_a, 2, IM, RE, far, True, True)
-        far_sub(2, acc_a, b_sb)
         passes(g2, 2, IM, IM, far, False, True)
         nc.scalar.activation(out=sq_re[2][:, 0:256], in_=g2[:, 0:256], func=SQUARE)
         t_banks((3, IM, 0), (3, IM, 1), (3, IM, 2), (3, IM, 3))
-        finish(2, 0, 256)
         mirror(1, P)
-        mirror(2, 2 * P)
         g3 = bank()
         passes(g3, 3, RE, RE, far, True, False)
         acc_b = bank()
         passes(acc_b, 3, RE, IM, far, True, True)
-        b_sb = copy_b(acc_b)
-        acc_a = bank()
-        passes(acc_a, 3, IM, RE, far, True, True)
-        far_sub(3, acc_a, b_sb)
+        b3_sb = copy_b(acc_b)
         passes(g3, 3, IM, IM, far, False, True)
         nc.scalar.activation(out=sq_re[3][:, 0:256], in_=g3[:, 0:256], func=SQUARE)
-        finish(3, 0, 256)
-        mirror(3, 2 * P)
 
         near = (2 * P, 4 * P)
-        a2 = bank()
-        passes(a2, 2, IM, RE, near, True, True)
-        nc.vector.tensor_copy(out=a_sb[2][:], in_=a2[:, 0:256])
         a3 = bank()
-        passes(a3, 3, IM, RE, near, True, True)
-        nc.scalar.copy(out=a_sb[3][:], in_=a3[:, 0:256])
+        passes(a3, 3, IM, RE, (0, N), True, True)
+        far_sub(3, a3, b3_sb)
+        nc.scalar.copy(out=a_sb[3][:], in_=a3[:, 256:512])
+        finish(3, 0, 256)
+        mirror(3, 2 * P)
+        a2 = bank()
+        passes(a2, 2, IM, RE, (0, N), True, True)
+        nc.vector.tensor_copy(out=a_sb[2][:], in_=a2[:, 256:512])
+        far_sub(2, a2, b2_sb)
+        finish(2, 0, 256)
+        mirror(2, 2 * P)
         g3 = bank()
         passes(g3, 3, RE, RE, near, True, False)
         ex = ex_bank()

from contextlib import ExitStack

import concourse.mybir as mybir
from concourse.masks import make_identity

F32 = mybir.dt.float32
BF16 = mybir.dt.bfloat16
U32 = mybir.dt.uint32
U8 = mybir.dt.uint8
FP8X4 = mybir.dt.float8_e4m3fn_x4
SQUARE = mybir.ActivationFunctionType.Square

P = 128
N = 512
D = 4096
TILES = N // P
PASSES = D // 512
CHUNKS = 4
FLOPS = 4 * 2 * N * N * D
RE, IM = 0, 1

HEAD_IDLE = 4
VECTOR_COPY = 1
LOADS = ((0, 1024), (1024, 2048), (2048, 3072), (3072, 4096))


def tile_quantumgraphneuralnetwork_pa_kernel(tc, latent_re, latent_im, out):
    nc = tc.nc
    latent = (latent_re, latent_im)
    with ExitStack() as ctx:
        keep = ctx.enter_context(tc.tile_pool(name="keep", bufs=1))
        stage = ctx.enter_context(tc.tile_pool(name="stage", bufs=8))
        epi = ctx.enter_context(tc.tile_pool(name="epi", bufs=2))
        psum = ctx.enter_context(tc.psum_pool(name="psum", bufs=1))
        ctx.enter_context(tc.manual_schedule())

        x_sb = [[keep.tile([P, D], BF16, name="x%d_%d" % (s, j)) for j in range(TILES)] for s in range(2)]
        codes = [keep.tile([P, PASSES, N], U32, name="codes%d" % s, align_bytes=64) for s in range(2)]
        scales = [keep.tile([P, PASSES, N], U8, name="scales%d" % s, align_bytes=64) for s in range(2)]
        out_sb = [keep.tile([P, N], F32, name="out_sb%d" % j, align_bytes=64) for j in range(TILES)]
        sq_re = [keep.tile([P, N], F32, name="sq_re%d" % j) for j in range(TILES)]
        sq_im = [keep.tile([P, N], F32, name="sq_im%d" % j) for j in range(TILES)]
        a_sb = [keep.tile([P, 2 * P], F32, name="a_sb%d" % j) for j in range(TILES)]
        ident = keep.tile([P, P], F32, name="ident")
        warm = keep.tile([P, 2], F32, name="warm")
        zeros = keep.tile([P, N], BF16, name="zeros")
        idle_acc = psum.tile([P, 4, P], F32, tag="tp", bufs=4, name="idle_acc")

        nc.vector.memset(zeros[:], 0.0)
        for i in range(HEAD_IDLE):
            nc.tensor.matmul(out=idle_acc[:].rearrange("p e n -> p (e n)"), lhsT=zeros[:, 0:P], rhs=zeros[:], start=True, stop=True)

        def load(s, j, c0, c1):
            nc.sync.dma_start(out=x_sb[s][j][:, c0:c1], in_=latent[s][P * j : P * j + P, c0:c1])

        for c0, c1 in LOADS:
            for s in range(2):
                for j in range(2):
                    load(s, j, c0, c1)
        load(RE, 2, 0, D // 2)
        load(RE, 2, D // 2, D)
        load(IM, 2, 0, D)
        load(RE, 3, 0, D)
        load(IM, 3, 0, D)

        make_identity(nc, ident[:])
        nc.vector.memset(warm[:, 0:1], 0.0)
        nc.scalar.activation(out=warm[:, 1:2], in_=warm[:, 0:1], func=SQUARE)

        def transposes(j, s, c, vector):
            words = x_sb[s][j][:].bitcast(F32)
            tp = psum.tile([P, 4, P], F32, tag="tp", bufs=4, name="tp")
            for q in range(4):
                w0 = 512 * c + P * q
                nc.tensor.transpose(tp[:, q, :], words[:, w0 : w0 + P], ident[:])
            grouped = stage.tile([P, 1024], BF16, tag="grouped", name="grouped", align_bytes=64)
            dst = grouped[:].bitcast(F32).rearrange("p (a n u) -> p a n u", a=2, u=2)
            src = tp[:].rearrange("p (a u) n -> p a n u", u=2)
            if vector:
                nc.vector.tensor_copy(out=dst, in_=src)
            else:
                nc.scalar.copy(out=dst, in_=src)
            return grouped

        def quantise(j, s, c, grouped):
            rows = slice(P * j, P * j + P)
            for a in range(2):
                g = 2 * c + a
                nc.vector.quantize_mx(
                    out=codes[s][:, g, rows].bitcast(FP8X4),
                    scales=scales[s][:, g, rows],
                    in_=grouped[:, 512 * a : 512 * a + 512],
                )

        def t_banks(*banks):
            held = None
            for i, bank in enumerate(banks):
                grouped = transposes(*bank, i % 3 == VECTOR_COPY)
                if held is not None:
                    quantise(*banks[i - 1], held)
                held = grouped
            quantise(*banks[-1], held)

        def passes(acc, j, stat, mov, span, first, last, gs=range(PASSES)):
            rows = slice(P * j, P * j + P)
            cols = slice(span[0], span[1])
            for g in gs:
                nc.tensor.matmul_mx(
                    out=acc[:, 0 : span[1] - span[0]],
                    lhsT=codes[stat][:, g, rows].bitcast(FP8X4),
                    lhsT_scale=scales[stat][:, g, rows],
                    rhs=codes[mov][:, g, cols].bitcast(FP8X4),
                    rhs_scale=scales[mov][:, g, cols],
                    start=(first and g == 0),
                    stop=(last and g == PASSES - 1),
                )

        def bank():
            return psum.tile([P, N], F32, tag="acc", bufs=4, name="acc")

        def ex_bank():
            return psum.tile([P, 4, P], F32, tag="tp", bufs=4, name="ex")

        def store(j, c0, c1):
            nc.sync.dma_start(out=out[P * j : P * j + P, c0:c1], in_=out_sb[j][:, c0:c1])

        def finish(j, c0, c1):
            nc.vector.tensor_add(out=out_sb[j][:, c0:c1], in0=sq_re[j][:, c0:c1], in1=sq_im[j][:, c0:c1])
            store(j, c0, c1)

        def mirror(j, width):
            turned = epi.tile([P, width], F32, tag="turned%d" % j, bufs=1, name="turned", align_bytes=64)
            nc.vector.transpose(turned[:], out_sb[j][:, 0:width])
            for q in range(4):
                nc.sync.dma_start(
                    out=out[0:width, P * j + 32 * q : P * j + 32 * q + 32].rearrange("(b c) r -> c b r", c=32),
                    in_=turned[32 * q : 32 * q + 32, :].rearrange("c (b r) -> c b r", r=32),
                )

        def a_turn(ex, j):
            nc.tensor.transpose(ex[:, 0, :], a_sb[j][:, P : 2 * P], ident[:])
            nc.tensor.transpose(ex[:, 1, :], a_sb[j + 1][:, P : 2 * P], ident[:])
            nc.tensor.transpose(ex[:, 2, :], a_sb[j][:, 0:P], ident[:])

        def a_square(ex, j):
            lo, mid, hi = P * j, P * j + P, P * j + 2 * P
            diff = epi.tile([P, 2, P], F32, tag="diff_pair", name="diff_pair")
            nc.vector.tensor_sub(
                out=diff[:], in0=a_sb[j + 1][:].rearrange("p (e n) -> p e n", e=2), in1=ex[:, 0:2, :]
            )
            diff_d = epi.tile([P, P], F32, tag="diff_d", name="diff_d")
            nc.vector.tensor_sub(out=diff_d[:], in0=a_sb[j][:, 0:P], in1=ex[:, 2, :])
            nc.scalar.activation(
                out=sq_im[j + 1][:, lo:hi].rearrange("p (e n) -> p e n", e=2), in_=diff[:], func=SQUARE
            )
            nc.vector.tensor_mul(out=sq_im[j][:, lo:mid], in0=diff_d[:], in1=diff_d[:])

        a0, a1, g1, g0 = bank(), bank(), bank(), bank()

        def pair_im(c):
            gs = range(2 * c, 2 * c + 2)
            passes(g1, 1, IM, IM, (0, 256), False, True, gs)
            passes(g0, 0, IM, IM, (0, 128), False, True, gs)

        def pair_rest(c):
            gs = range(2 * c, 2 * c + 2)
            passes(g1, 1, RE, RE, (0, 256), True, False, gs)
            passes(g0, 0, RE, RE, (0, 128), True, False, gs)
            passes(a1, 1, IM, RE, (0, 256), True, True, gs)
            passes(a0, 0, IM, RE, (0, 256), True, True, gs)

        t_banks((0, RE, 0), (1, RE, 0))
        t_banks((0, IM, 0), (1, IM, 0))
        t_banks((0, RE, 1), (1, RE, 1))
        pair_rest(0)
        t_banks((0, IM, 1), (1, IM, 1), (0, RE, 2), (1, RE, 2))
        pair_im(0)
        pair_rest(1)
        t_banks((0, IM, 2), (1, IM, 2), (0, RE, 3), (1, RE, 3))
        pair_im(1)
        pair_rest(2)
        t_banks((0, IM, 3), (1, IM, 3), (2, RE, 0), (2, RE, 1))
        pair_im(2)
        pair_rest(3)
        pair_im(3)
        nc.vector.tensor_copy(out=a_sb[0][:], in_=a0[:, 0:256])
        nc.scalar.copy(out=a_sb[1][:], in_=a1[:, 0:256])
        t_banks((2, RE, 2), (2, RE, 3), (2, IM, 0), (2, IM, 1), (2, IM, 2))
        nc.scalar.activation(out=sq_re[1][:, 0:256], in_=g1[:, 0:256], func=SQUARE)
        nc.scalar.activation(out=sq_re[0][:, 0:128], in_=g0[:, 0:128], func=SQUARE)

        far = (0, 2 * P)

        def copy_b(acc_b):
            b_sb = epi.tile([P, 2 * P], F32, tag="b_sb", name="b_sb")
            nc.scalar.copy(out=b_sb[:], in_=acc_b[:, 0:256])
            return b_sb

        def far_sub(j, acc_a, b_sb):
            diff = epi.tile([P, 2 * P], F32, tag="diff", name="diff")
            nc.vector.tensor_sub(out=diff[:], in0=acc_a[:, 0:256], in1=b_sb[:])
            nc.scalar.activation(out=sq_im[j][:, 0:256], in_=diff[:], func=SQUARE)

        g2 = bank()
        passes(g2, 2, RE, RE, far, True, False)
        acc_b = bank()
        passes(acc_b, 2, RE, IM, far, True, True, range(0, 6))
        t_banks((2, IM, 3), (3, RE, 0), (3, RE, 1), (3, RE, 2), (3, RE, 3))
        ex = ex_bank()
        a_turn(ex, 0)
        passes(acc_b, 2, RE, IM, far, True, True, range(6, 8))
        b2_sb = copy_b(acc_b)
        a_square(ex, 0)
        finish(1, 0, 256)
        finish(0, 0, 128)
        passes(g2, 2, IM, IM, far, False, True)
        nc.scalar.activation(out=sq_re[2][:, 0:256], in_=g2[:, 0:256], func=SQUARE)
        t_banks((3, IM, 0), (3, IM, 1), (3, IM, 2), (3, IM, 3))
        mirror(1, P)
        g3 = bank()
        passes(g3, 3, RE, RE, far, True, False)
        acc_b = bank()
        passes(acc_b, 3, RE, IM, far, True, True)
        b3_sb = copy_b(acc_b)
        passes(g3, 3, IM, IM, far, False, True)
        nc.scalar.activation(out=sq_re[3][:, 0:256], in_=g3[:, 0:256], func=SQUARE)

        near = (2 * P, 4 * P)
        a3 = bank()
        passes(a3, 3, IM, RE, (0, N), True, True)
        far_sub(3, a3, b3_sb)
        nc.scalar.copy(out=a_sb[3][:], in_=a3[:, 256:512])
        finish(3, 0, 256)
        mirror(3, 2 * P)
        a2 = bank()
        passes(a2, 2, IM, RE, (0, N), True, True)
        nc.vector.tensor_copy(out=a_sb[2][:], in_=a2[:, 256:512])
        far_sub(2, a2, b2_sb)
        finish(2, 0, 256)
        mirror(2, 2 * P)
        g3 = bank()
        passes(g3, 3, RE, RE, near, True, False)
        ex = ex_bank()
        a_turn(ex, 2)
        a_square(ex, 2)
        passes(g3, 3, IM, IM, near, False, True)
        nc.scalar.activation(out=sq_re[3][:, 256:384], in_=g3[:, 0:128], func=SQUARE)
        nc.vector.tensor_add(out=out_sb[3][:, 256:384], in0=sq_re[3][:, 256:384], in1=sq_im[3][:, 256:384])
        nc.scalar.activation(out=sq_re[3][:, 384:512], in_=g3[:, 128:256], func=SQUARE)
        nc.vector.tensor_add(out=out_sb[3][:, 384:512], in0=sq_re[3][:, 384:512], in1=sq_im[3][:, 384:512])
        store(3, 256, 512)
        g2 = bank()
        diag = (2 * P, 3 * P)
        passes(g2, 2, RE, RE, diag, True, False)
        passes(g2, 2, IM, IM, diag, False, True)
        ex = ex_bank()
        nc.tensor.transpose(ex[:, 0, :], out_sb[3][:, 256:384], ident[:])
        nc.scalar.activation(out=sq_re[2][:, 256:384], in_=g2[:, 0:128], func=SQUARE)
        finish(2, 256, 384)
        m_sb = epi.tile([P, P], F32, tag="m_sb", name="m_sb")
        nc.scalar.copy(out=m_sb[:], in_=ex[:, 0, :])
        nc.sync.dma_start(out=out[256:384, 384:512], in_=m_sb[:])
